import numpy as np
import ml_dtypes


def mxq(x, axis, fmt="e4m3"):
    dtype, down = {"e4m3": (ml_dtypes.float8_e4m3fn, 7), "e5m2": (ml_dtypes.float8_e5m2, 14)}[fmt]
    v = np.moveaxis(np.asarray(x, np.float32).astype(ml_dtypes.bfloat16).astype(np.float64), axis, -1)
    blocks = v.reshape(v.shape[:-1] + (-1, 32))
    amax = np.abs(blocks).max(-1, keepdims=True)
    byte = np.maximum(np.where(amax > 0, np.frexp(amax)[1] - 1 + 127, 0) - down, 1)
    scale = np.exp2(byte - 127.0)
    codes = (blocks / scale).astype(np.float32).astype(dtype).astype(np.float64)
    return np.moveaxis((codes * scale).reshape(v.shape), -1, axis)


WIDE = False


def mx_kscale(k):
    if not WIDE:
        return np.ones(k)
    levels = np.array([10, -10, 5, -5, 0])
    a = np.random.permutation(np.resize(levels, k // 512 * 4)).reshape(k // 512, 4)
    idx = np.arange(k)
    return np.exp2(a[idx // 512, idx % 128 // 32])


BF16 = ml_dtypes.bfloat16


def bf(x):
    return np.asarray(x, np.float32).astype(BF16)


def f64(x):
    return np.asarray(x).astype(np.float64)


B, N, D, H, DH = 8, 512, 1024, 4, 128
EPS = 1e-5


def rotate_every_two(u):
    p = u.reshape(u.shape[:-1] + (-1, 2))
    return np.stack((-p[..., 1], p[..., 0]), axis=-1).reshape(u.shape)


def apply_rotary(u, sin, cos):
    return u * cos + rotate_every_two(u) * sin


def setup_inputs():
    s = mx_kscale(D)
    r = np.exp2(-np.random.uniform(0.0, 9.0, (B, N, 1)))
    inv_freq = 1.0 / 10000.0 ** (np.arange(0, DH, 2) / DH)
    freqs = np.repeat(np.arange(N)[:, None] * inv_freq[None, :], 2, axis=-1)
    return {"x": bf((np.random.standard_normal((B, N, D)) + 0.5) * r),
            "gamma": bf((1.0 + 0.1 * np.random.standard_normal(D)) * s),
            "wq": bf(np.random.standard_normal((D, H * DH)) * 2.0 / np.sqrt(D) / s[:, None]),
            "wk": bf(np.random.standard_normal((D, DH)) / np.sqrt(D) / s[:, None]),
            "wv": bf(np.random.standard_normal((D, DH)) / np.sqrt(D) / s[:, None]),
            "sin": bf(np.sin(freqs)), "cos": bf(np.cos(freqs))}


def reference(x, gamma, wq, wk, wv, sin, cos):
    x, sin, cos = f64(x), f64(sin), f64(cos)
    mean = x.mean(-1, keepdims=True)
    var = np.square(x).mean(-1, keepdims=True) - np.square(mean)
    xn = 1.0 / np.sqrt(var + EPS) * (x - mean) * f64(gamma)
    xq = mxq(xn, 2, "e4m3")
    q = xq @ mxq(f64(wq), 0, "e4m3")
    k = xq @ mxq(f64(wk), 0, "e4m3")
    v = xq @ mxq(f64(wv), 0, "e4m3")
    q = q.reshape(B, N, H, DH).transpose(0, 2, 1, 3) * DH ** -0.5
    return apply_rotary(q, sin, cos), apply_rotary(k, sin, cos), v

@@ -1,0 +1,301 @@
+from contextlib import ExitStack
+
+import concourse.mybir as mybir
+from concourse.masks import make_identity
+
+FP32 = mybir.dt.float32
+BF16 = mybir.dt.bfloat16
+U32 = mybir.dt.uint32
+U8 = mybir.dt.uint8
+FP8X4 = mybir.dt.float8_e4m3fn_x4
+ALU = mybir.AluOpType
+ACT = mybir.ActivationFunctionType
+
+B, N, D, H, DH = 8, 512, 1024, 4, 128
+EPS = 1e-5
+Q_SCALE = DH**-0.5
+
+P = 128
+PACK = 4
+PASSES = D // (P * PACK)
+K_BLOCKS = D // P
+TILES = N // P
+ROW_TILES = B * TILES
+HEADS = H + 1
+HALF = DH // 2
+Q_COLS = slice(0, H * DH)
+K_COLS = slice(H * DH, H * DH + DH)
+V_COLS = slice(H * DH + DH, H * DH + 2 * DH)
+KV_COLS = slice(H * DH, H * DH + 2 * DH)
+W_COLS = H * DH + 2 * DH
+
+SUM_LEAD = 7
+STAT_LEAD = 4
+Y_LEAD = 3
+XT_LEAD = 1
+
+FLOPS = 2 * B * N * D * W_COLS
+
+
+def tile_attention_pa_t_kernel(tc, x, gamma, wq, wk, wv, sin, cos, out_0, out_1, out_2):
+    nc = tc.nc
+    with ExitStack() as ctx:
+        const = ctx.enter_context(tc.tile_pool(name="const", bufs=1))
+        x_pool = ctx.enter_context(tc.tile_pool(name="x_pool", bufs=B))
+        stat_pool = ctx.enter_context(tc.tile_pool(name="stat_pool", bufs=3))
+        unread_pool = ctx.enter_context(tc.tile_pool(name="unread_pool", bufs=4))
+        y_pool = ctx.enter_context(tc.tile_pool(name="y_pool", bufs=4))
+        mx_pool = ctx.enter_context(tc.tile_pool(name="mx_pool", bufs=3))
+        out_pool = ctx.enter_context(tc.tile_pool(name="out_pool", bufs=2))
+        xt_psum = ctx.enter_context(tc.psum_pool(name="xt_psum", bufs=4))
+        qk_psum = ctx.enter_context(tc.psum_pool(name="qk_psum", bufs=1))
+        v_psum = ctx.enter_context(tc.psum_pool(name="v_psum", bufs=2))
+
+        ident = const.tile([P, P], FP32)
+        make_identity(nc, ident[:])
+
+        ctx.enter_context(tc.manual_schedule())
+
+        x_sb = [x_pool.tile([P, TILES, D], BF16, name="x_sb") for b in range(B)]
+
+        def load_x(b):
+            nc.sync.dma_start(out=x_sb[b][:], in_=x[b].rearrange("(p t) k -> p t k", t=TILES))
+
+        load_x(0)
+        w_raw = const.tile([P, K_BLOCKS, W_COLS], BF16)
+        nc.sync.dma_start(out=w_raw[:, :, Q_COLS], in_=wq.rearrange("(j p) n -> p j n", p=P))
+        nc.sync.dma_start(out=w_raw[:, :, K_COLS], in_=wk.rearrange("(j p) n -> p j n", p=P))
+        nc.sync.dma_start(out=w_raw[:, :, V_COLS], in_=wv.rearrange("(j p) n -> p j n", p=P))
+        gamma_rows = const.tile([P, P], BF16)
+        nc.vector.memset(gamma_rows[:], 0.0)
+        nc.sync.dma_start(out=gamma_rows[0:K_BLOCKS, :], in_=gamma.rearrange("(j p) -> j p", p=P))
+        cos_bf = const.tile([P, TILES, DH], BF16)
+        sin_bf = const.tile([P, TILES, DH], BF16)
+        nc.sync.dma_start(out=cos_bf[:], in_=cos.rearrange("(p t) d -> p t d", t=TILES))
+        nc.sync.dma_start(out=sin_bf[:], in_=sin.rearrange("(p t) d -> p t d", t=TILES))
+        for b in range(1, B):
+            load_x(b)
+
+        one = const.tile([P, 1], FP32)
+        nc.vector.memset(one[:], 1.0)
+        root_of_one = const.tile([P, 1], FP32)
+        nc.scalar.activation(out=root_of_one[:], in_=one[:], func=ACT.Sqrt)
+
+        gamma_rows_f = const.tile([P, P], FP32)
+        nc.vector.tensor_copy(out=gamma_rows_f[:], in_=gamma_rows[:])
+        gamma_ps = xt_psum.tile([P, PACK, P], FP32, name="xt")
+        nc.tensor.transpose(gamma_ps[:, 0, :], gamma_rows_f[:], ident[:])
+        gamma_col = const.tile([P, K_BLOCKS], FP32)
+        nc.vector.tensor_copy(out=gamma_col[:], in_=gamma_ps[:, 0, 0:K_BLOCKS])
+
+        cos_q = const.tile([P, TILES, DH], FP32)
+        nc.gpsimd.tensor_scalar(out=cos_q[:], in0=cos_bf[:], scalar1=Q_SCALE, scalar2=0.0, op0=ALU.mult, op1=ALU.add)
+        sin_q = const.tile([P, TILES, 2, HALF], FP32)
+        sin_k = const.tile([P, TILES, 2, HALF], FP32)
+        sin_pairs = sin_bf[:].rearrange("p t (i m) -> p t i m", m=2)
+        for table, factor in ((sin_q, Q_SCALE), (sin_k, 1.0)):
+            nc.gpsimd.tensor_scalar(
+                out=table[:, :, 0, :], in0=sin_pairs[:, :, :, 0], scalar1=-factor, scalar2=0.0, op0=ALU.mult, op1=ALU.add
+            )
+            nc.gpsimd.tensor_scalar(
+                out=table[:, :, 1, :], in0=sin_pairs[:, :, :, 1], scalar1=factor, scalar2=0.0, op0=ALU.mult, op1=ALU.add
+            )
+
+        w_codes = const.tile([P, PASSES, W_COLS], U32, align_bytes=64)
+        w_scales = const.tile([P, PASSES, W_COLS], U8, align_bytes=64)
+        w_grouped = [const.tile([P, W_COLS, PACK], BF16, name="w_grouped%d" % g, align_bytes=64) for g in range(PASSES)]
+        for g in range(PASSES):
+            nc.vector.tensor_copy(
+                out=w_grouped[g][:], in_=w_raw[:, g * PACK : (g + 1) * PACK, :].rearrange("p j n -> p n j")
+            )
+        for g in range(PASSES):
+            for cols in (Q_COLS, KV_COLS):
+                nc.vector.quantize_mx(
+                    out=w_codes[:, g, cols].bitcast(FP8X4),
+                    scales=w_scales[:, g, cols],
+                    in_=w_grouped[g][:, cols, :].rearrange("p n j -> p (n j)"),
+                )
+
+        sums = {}
+        squares = {}
+
+        def row_sums(i):
+            b, t = divmod(i, TILES)
+            if t == 0:
+                sums[b] = stat_pool.tile([P, TILES], FP32, name="sums")
+                squares[b] = stat_pool.tile([P, TILES], FP32, name="squares")
+            for func, total in ((ACT.Square, squares[b]), (ACT.Identity, sums[b])):
+                unread = unread_pool.tile([P, D], BF16, name="unread")
+                nc.scalar.activation(out=unread[:], in_=x_sb[b][:, t, :], func=func, accum_out=total[:, t : t + 1])
+
+        neg_mean = {}
+        std = {}
+        rstd = {}
+
+        def variance(b):
+            neg_mean[b] = stat_pool.tile([P, TILES], FP32, name="neg_mean")
+            nc.vector.tensor_scalar_mul(out=neg_mean[b][:], in0=sums[b][:], scalar1=-1.0 / D)
+            mean_sq = stat_pool.tile([P, TILES], FP32, name="mean_sq")
+            nc.vector.tensor_tensor(out=mean_sq[:], in0=neg_mean[b][:], in1=neg_mean[b][:], op=ALU.mult)
+            second = stat_pool.tile([P, TILES], FP32, name="second")
+            nc.vector.tensor_scalar(
+                out=second[:], in0=squares[b][:], scalar1=1.0 / D, scalar2=EPS, op0=ALU.mult, op1=ALU.add
+            )
+            var_eps = stat_pool.tile([P, TILES], FP32, name="var_eps")
+            nc.vector.tensor_tensor(out=var_eps[:], in0=second[:], in1=mean_sq[:], op=ALU.subtract)
+            std[b] = stat_pool.tile([P, TILES], FP32, name="std")
+            nc.scalar.activation(out=std[b][:], in_=var_eps[:], func=ACT.Sqrt)
+
+        def inverse_std(b):
+            rstd[b] = stat_pool.tile([P, TILES], FP32, name="rstd")
+            nc.vector.reciprocal(out=rstd[b][:], in_=std[b][:])
+
+        y = {}
+
+        def normalise(i):
+            b, t = divmod(i, TILES)
+            y[i] = y_pool.tile([P, D], FP32, name="y")
+            nc.gpsimd.tensor_scalar(
+                out=y[i][:],
+                in0=x_sb[b][:, t, :],
+                scalar1=neg_mean[b][:, t : t + 1],
+                scalar2=rstd[b][:, t : t + 1],
+                op0=ALU.add,
+                op1=ALU.mult,
+            )
+
+        grouped = {}
+
+        def transpose_and_scale(i):
+            grouped[i] = mx_pool.tile([P, PASSES, P, PACK], BF16, name="grouped", align_bytes=64)
+            xt = [xt_psum.tile([P, PACK, P], FP32, name="xt") for g in range(PASSES)]
+            for g in range(PASSES):
+                for j in range(PACK):
+                    block = g * PACK + j
+                    nc.tensor.transpose(xt[g][:, j, :], y[i][:, block * P : (block + 1) * P], ident[:])
+            for g in range(PASSES):
+                nc.vector.tensor_tensor(
+                    out=grouped[i][:, g, :, :],
+                    in0=xt[g][:].rearrange("p j r -> p r j"),
+                    in1=gamma_col[:, g * PACK : (g + 1) * PACK].unsqueeze(1).to_broadcast([P, P, PACK]),
+                    op=ALU.mult,
+                )
+
+        codes = {}
+        scales = {}
+
+        def quantise(i):
+            codes[i] = mx_pool.tile([P, PASSES, P], U32, name="codes", align_bytes=64)
+            scales[i] = mx_pool.tile([P, PASSES, P], U8, name="scales", align_bytes=64)
+            nc.vector.quantize_mx(
+                out=codes[i][:].rearrange("p g r -> p (g r)").bitcast(FP8X4),
+                scales=scales[i][:].rearrange("p g r -> p (g r)"),
+                in_=grouped[i][:].rearrange("p g r j -> p (g r j)"),
+            )
+
+        q_ps = {}
+        k_ps = {}
+        v_ps = {}
+
+        def project(i):
+            b, t = divmod(i, TILES)
+            q_ps[i] = qk_psum.tile([P, H * DH], FP32, name="q_ps")
+            if t == 0:
+                k_ps[b] = qk_psum.tile([P, TILES, DH], FP32, name="k_ps")
+                v_ps[b] = v_psum.tile([P, TILES, DH], FP32, name="v_ps")
+            for acc, cols in ((q_ps[i][:], Q_COLS), (k_ps[b][:, t, :], K_COLS), (v_ps[b][:, t, :], V_COLS)):
+                for g in range(PASSES):
+                    nc.tensor.matmul_mx(
+                        out=acc,
+                        lhsT=codes[i][:, g, :].bitcast(FP8X4),
+                        lhsT_scale=scales[i][:, g, :],
+                        rhs=w_codes[:, g, cols].bitcast(FP8X4),
+                        rhs_scale=w_scales[:, g, cols],
+                        start=(g == 0),
+                        stop=(g == PASSES - 1),
+                    )
+
+        rotated = {}
+        sin_part = {}
+
+        def rotary_products(u, cos_table, sin_table, cos_out, sin_out):
+            nc.vector.tensor_tensor(out=cos_out, in0=u, in1=cos_table, op=ALU.mult)
+            pairs = u.rearrange("p a (i m) -> p a i m", m=2)
+            for plane in range(2):
+                nc.vector.tensor_tensor(
+                    out=sin_out[:, :, plane, :], in0=pairs[:, :, :, 1 - plane], in1=sin_table[:, :, plane, :], op=ALU.mult
+                )
+
+        def rotary_sum(cos_out, sin_out):
+            interleaved = cos_out.rearrange("p a (i m) -> p a i m", m=2)
+            nc.gpsimd.tensor_tensor(
+                out=interleaved, in0=interleaved, in1=sin_out.rearrange("p a m i -> p a i m"), op=ALU.add
+            )
+
+        def rotate_q(i):
+            b, t = divmod(i, TILES)
+            if t == 0:
+                rotated[b] = out_pool.tile([P, HEADS, TILES, DH], FP32, name="rotated")
+                sin_part[b] = out_pool.tile([P, HEADS, TILES, 2, HALF], FP32, name="sin_part")
+            rotary_products(
+                u=q_ps[i][:].rearrange("p (h d) -> p h d", h=H),
+                cos_table=cos_q[:, t, :].unsqueeze(1).to_broadcast([P, H, DH]),
+                sin_table=sin_q[:, t, :, :].unsqueeze(1).to_broadcast([P, H, 2, HALF]),
+                cos_out=rotated[b][:, 0:H, t, :],
+                sin_out=sin_part[b][:, 0:H, t, :, :],
+            )
+
+        def sum_q(i):
+            b, t = divmod(i, TILES)
+            rotary_sum(rotated[b][:, 0:H, t, :], sin_part[b][:, 0:H, t, :, :])
+
+        v_sb = {}
+
+        def rotate_k_copy_v(b):
+            rotary_products(
+                u=k_ps[b][:],
+                cos_table=cos_bf[:],
+                sin_table=sin_k[:],
+                cos_out=rotated[b][:, H, :, :],
+                sin_out=sin_part[b][:, H, :, :, :],
+            )
+            v_sb[b] = out_pool.tile([P, TILES, DH], FP32, name="v_sb")
+            nc.scalar.copy(out=v_sb[b][:], in_=v_ps[b][:])
+
+        def sum_k_and_store(b):
+            rotary_sum(rotated[b][:, H, :, :], sin_part[b][:, H, :, :, :])
+            nc.sync.dma_start(out=out_0[b].rearrange("h (p t) d -> p h t d", t=TILES), in_=rotated[b][:, 0:H, :, :])
+            nc.sync.dma_start(out=out_1[b].rearrange("(p t) d -> p t d", t=TILES), in_=rotated[b][:, H, :, :])
+            nc.sync.dma_start(out=out_2[b].rearrange("(p t) d -> p t d", t=TILES), in_=v_sb[b][:])
+
+        def is_tile(i):
+            return 0 <= i < ROW_TILES
+
+        def starts_entry(i):
+            return is_tile(i) and i % TILES == 0
+
+        def ends_entry(i):
+            return is_tile(i) and i % TILES == TILES - 1
+
+        for s in range(-SUM_LEAD, ROW_TILES + 1):
+            if is_tile(s - 1):
+                sum_q(s - 1)
+            if ends_entry(s - 1):
+                sum_k_and_store((s - 1) // TILES)
+            if is_tile(s + SUM_LEAD):
+                row_sums(s + SUM_LEAD)
+            if is_tile(s + XT_LEAD):
+                transpose_and_scale(s + XT_LEAD)
+            if starts_entry(s + STAT_LEAD - 1):
+                inverse_std((s + STAT_LEAD - 1) // TILES)
+            if is_tile(s + Y_LEAD):
+                normalise(s + Y_LEAD)
+            if is_tile(s):
+                project(s)
+                rotate_q(s)
+            if ends_entry(s):
+                rotate_k_copy_v(s // TILES)
+            if is_tile(s + XT_LEAD):
+                quantise(s + XT_LEAD)
+            if starts_entry(s + STAT_LEAD):
+                variance((s + STAT_LEAD) // TILES)

@@ -29,10 +29,13 @@ V_COLS = slice(H * DH + DH, H * DH + 2 * DH)
 KV_COLS = slice(H * DH, H * DH + 2 * DH)
 W_COLS = H * DH + 2 * DH
 
-SUM_LEAD = 7
-STAT_LEAD = 4
-Y_LEAD = 3
-XT_LEAD = 1
+SUM_LEAD = 8
+STAT_LEAD = 5
+Y_LEAD = 4
+T_LEAD = 3
+G_LEAD = 2
+MX_LEAD = 1
+VECTOR_SUM_ENTRIES = 1
 
 FLOPS = 2 * B * N * D * W_COLS
 
@@ -47,9 +50,8 @@ def tile_attention_pa_t_kernel(tc, x, gamma, wq, wk, wv, sin, cos, out_0, out_1,
         y_pool = ctx.enter_context(tc.tile_pool(name="y_pool", bufs=4))
         mx_pool = ctx.enter_context(tc.tile_pool(name="mx_pool", bufs=3))
         out_pool = ctx.enter_context(tc.tile_pool(name="out_pool", bufs=2))
-        xt_psum = ctx.enter_context(tc.psum_pool(name="xt_psum", bufs=4))
-        qk_psum = ctx.enter_context(tc.psum_pool(name="qk_psum", bufs=1))
-        v_psum = ctx.enter_context(tc.psum_pool(name="v_psum", bufs=2))
+        xt_psum = ctx.enter_context(tc.psum_pool(name="xt_psum", bufs=2))
+        qkv_psum = ctx.enter_context(tc.psum_pool(name="qkv_psum", bufs=2))
 
         ident = const.tile([P, P], FP32)
         make_identity(nc, ident[:])
@@ -62,6 +64,7 @@ def tile_attention_pa_t_kernel(tc, x, gamma, wq, wk, wv, sin, cos, out_0, out_1,
             nc.sync.dma_start(out=x_sb[b][:], in_=x[b].rearrange("(p t) k -> p t k", t=TILES))
 
         load_x(0)
+        load_x(1)
         w_raw = const.tile([P, K_BLOCKS, W_COLS], BF16)
         nc.sync.dma_start(out=w_raw[:, :, Q_COLS], in_=wq.rearrange("(j p) n -> p j n", p=P))
         nc.sync.dma_start(out=w_raw[:, :, K_COLS], in_=wk.rearrange("(j p) n -> p j n", p=P))
@@ -73,20 +76,13 @@ def tile_attention_pa_t_kernel(tc, x, gamma, wq, wk, wv, sin, cos, out_0, out_1,
         sin_bf = const.tile([P, TILES, DH], BF16)
         nc.sync.dma_start(out=cos_bf[:], in_=cos.rearrange("(p t) d -> p t d", t=TILES))
         nc.sync.dma_start(out=sin_bf[:], in_=sin.rearrange("(p t) d -> p t d", t=TILES))
-        for b in range(1, B):
+        for b in range(2, B):
             load_x(b)
 
         one = const.tile([P, 1], FP32)
         nc.vector.memset(one[:], 1.0)
         root_of_one = const.tile([P, 1], FP32)
         nc.scalar.activation(out=root_of_one[:], in_=one[:], func=ACT.Sqrt)
-
-        gamma_rows_f = const.tile([P, P], FP32)
-        nc.vector.tensor_copy(out=gamma_rows_f[:], in_=gamma_rows[:])
-        gamma_ps = xt_psum.tile([P, PACK, P], FP32, name="xt")
-        nc.tensor.transpose(gamma_ps[:, 0, :], gamma_rows_f[:], ident[:])
-        gamma_col = const.tile([P, K_BLOCKS], FP32)
-        nc.vector.tensor_copy(out=gamma_col[:], in_=gamma_ps[:, 0, 0:K_BLOCKS])
 
         cos_q = const.tile([P, TILES, DH], FP32)
         nc.gpsimd.tensor_scalar(out=cos_q[:], in0=cos_bf[:], scalar1=Q_SCALE, scalar2=0.0, op0=ALU.mult, op1=ALU.add)
@@ -101,20 +97,30 @@ def tile_attention_pa_t_kernel(tc, x, gamma, wq, wk, wv, sin, cos, out_0, out_1,
                 out=table[:, :, 1, :], in0=sin_pairs[:, :, :, 1], scalar1=factor, scalar2=0.0, op0=ALU.mult, op1=ALU.add
             )
 
+        gamma_col = const.tile([P, K_BLOCKS], FP32)
         w_codes = const.tile([P, PASSES, W_COLS], U32, align_bytes=64)
         w_scales = const.tile([P, PASSES, W_COLS], U8, align_bytes=64)
-        w_grouped = [const.tile([P, W_COLS, PACK], BF16, name="w_grouped%d" % g, align_bytes=64) for g in range(PASSES)]
-        for g in range(PASSES):
-            nc.vector.tensor_copy(
-                out=w_grouped[g][:], in_=w_raw[:, g * PACK : (g + 1) * PACK, :].rearrange("p j n -> p n j")
-            )
-        for g in range(PASSES):
-            for cols in (Q_COLS, KV_COLS):
-                nc.vector.quantize_mx(
-                    out=w_codes[:, g, cols].bitcast(FP8X4),
-                    scales=w_scales[:, g, cols],
-                    in_=w_grouped[g][:, cols, :].rearrange("p n j -> p (n j)"),
+
+        def prepare_gamma_and_weights():
+            gamma_rows_f = const.tile([P, P], FP32)
+            nc.vector.tensor_copy(out=gamma_rows_f[:], in_=gamma_rows[:])
+            gamma_ps = xt_psum.tile([P, PACK, P], FP32, name="xt")
+            nc.tensor.transpose(gamma_ps[:, 0, :], gamma_rows_f[:], ident[:])
+            nc.vector.tensor_copy(out=gamma_col[:], in_=gamma_ps[:, 0, 0:K_BLOCKS])
+            w_grouped = [
+                const.tile([P, W_COLS, PACK], BF16, name="w_grouped%d" % g, align_bytes=64) for g in range(PASSES)
+            ]
+            for g in range(PASSES):
+                nc.vector.tensor_copy(
+                    out=w_grouped[g][:], in_=w_raw[:, g * PACK : (g + 1) * PACK, :].rearrange("p j n -> p n j")
                 )
+            for g in range(PASSES):
+                for cols in (Q_COLS, KV_COLS):
+                    nc.vector.quantize_mx(
+                        out=w_codes[:, g, cols].bitcast(FP8X4),
+                        scales=w_scales[:, g, cols],
+                        in_=w_grouped[g][:, cols, :].rearrange("p n j -> p (n j)"),
+                    )
 
         sums = {}
         squares = {}
@@ -124,7 +130,10 @@ def tile_attention_pa_t_kernel(tc, x, gamma, wq, wk, wv, sin, cos, out_0, out_1,
             if t == 0:
                 sums[b] = stat_pool.tile([P, TILES], FP32, name="sums")
                 squares[b] = stat_pool.tile([P, TILES], FP32, name="squares")
-            for func, total in ((ACT.Square, squares[b]), (ACT.Identity, sums[b])):
+                if b < VECTOR_SUM_ENTRIES:
+                    nc.vector.tensor_reduce(out=sums[b][:], in_=x_sb[b][:], axis=mybir.AxisListType.X, op=ALU.add)
+            scalar_work = [(ACT.Square, squares[b])] + ([(ACT.Identity, sums[b])] if b >= VECTOR_SUM_ENTRIES else [])
+            for func, total in scalar_work:
                 unread = unread_pool.tile([P, D], BF16, name="unread")
                 nc.scalar.activation(out=unread[:], in_=x_sb[b][:, t, :], func=func, accum_out=total[:, t : t + 1])
 
@@ -164,19 +173,22 @@ def tile_attention_pa_t_kernel(tc, x, gamma, wq, wk, wv, sin, cos, out_0, out_1,
                 op1=ALU.mult,
             )
 
+        xt = {}
         grouped = {}
 
-        def transpose_and_scale(i):
-            grouped[i] = mx_pool.tile([P, PASSES, P, PACK], BF16, name="grouped", align_bytes=64)
-            xt = [xt_psum.tile([P, PACK, P], FP32, name="xt") for g in range(PASSES)]
+        def transpose(i):
+            xt[i] = [xt_psum.tile([P, PACK, P], FP32, name="xt") for g in range(PASSES)]
             for g in range(PASSES):
                 for j in range(PACK):
                     block = g * PACK + j
-                    nc.tensor.transpose(xt[g][:, j, :], y[i][:, block * P : (block + 1) * P], ident[:])
+                    nc.tensor.transpose(xt[i][g][:, j, :], y[i][:, block * P : (block + 1) * P], ident[:])
+
+        def scale_by_gamma(i):
+            grouped[i] = mx_pool.tile([P, PASSES, P, PACK], BF16, name="grouped", align_bytes=64)
             for g in range(PASSES):
                 nc.vector.tensor_tensor(
                     out=grouped[i][:, g, :, :],
-                    in0=xt[g][:].rearrange("p j r -> p r j"),
+                    in0=xt[i][g][:].rearrange("p j r -> p r j"),
                     in1=gamma_col[:, g * PACK : (g + 1) * PACK].unsqueeze(1).to_broadcast([P, P, PACK]),
                     op=ALU.mult,
                 )
@@ -199,10 +211,10 @@ def tile_attention_pa_t_kernel(tc, x, gamma, wq, wk, wv, sin, cos, out_0, out_1,
 
         def project(i):
             b, t = divmod(i, TILES)
-            q_ps[i] = qk_psum.tile([P, H * DH], FP32, name="q_ps")
+            q_ps[i] = qkv_psum.tile([P, H * DH], FP32, name="q_ps")
             if t == 0:
-                k_ps[b] = qk_psum.tile([P, TILES, DH], FP32, name="k_ps")
-                v_ps[b] = v_psum.tile([P, TILES, DH], FP32, name="v_ps")
+                k_ps[b] = qkv_psum.tile([P, TILES, DH], FP32, name="k_ps")
+                v_ps[b] = qkv_psum.tile([P, TILES, DH], FP32, name="v_ps")
             for acc, cols in ((q_ps[i][:], Q_COLS), (k_ps[b][:, t, :], K_COLS), (v_ps[b][:, t, :], V_COLS)):
                 for g in range(PASSES):
                     nc.tensor.matmul_mx(
@@ -284,18 +296,23 @@ def tile_attention_pa_t_kernel(tc, x, gamma, wq, wk, wv, sin, cos, out_0, out_1,
                 sum_k_and_store((s - 1) // TILES)
             if is_tile(s + SUM_LEAD):
                 row_sums(s + SUM_LEAD)
-            if is_tile(s + XT_LEAD):
-                transpose_and_scale(s + XT_LEAD)
+            if is_tile(s + MX_LEAD):
+                project(s + MX_LEAD)
+            if is_tile(s + G_LEAD):
+                scale_by_gamma(s + G_LEAD)
+            if is_tile(s + T_LEAD):
+                transpose(s + T_LEAD)
             if starts_entry(s + STAT_LEAD - 1):
                 inverse_std((s + STAT_LEAD - 1) // TILES)
             if is_tile(s + Y_LEAD):
                 normalise(s + Y_LEAD)
+            if s + Y_LEAD == 0:
+                prepare_gamma_and_weights()
             if is_tile(s):
-                project(s)
                 rotate_q(s)
             if ends_entry(s):
                 rotate_k_copy_v(s // TILES)
-            if is_tile(s + XT_LEAD):
-                quantise(s + XT_LEAD)
+            if is_tile(s + G_LEAD):
+                quantise(s + G_LEAD)
             if starts_entry(s + STAT_LEAD):
                 variance((s + STAT_LEAD) // TILES)

@@ -86,16 +86,19 @@ def tile_attention_pa_t_kernel(tc, x, gamma, wq, wk, wv, sin, cos, out_0, out_1,
 
         cos_q = const.tile([P, TILES, DH], FP32)
         nc.gpsimd.tensor_scalar(out=cos_q[:], in0=cos_bf[:], scalar1=Q_SCALE, scalar2=0.0, op0=ALU.mult, op1=ALU.add)
-        sin_q = const.tile([P, TILES, 2, HALF], FP32)
-        sin_k = const.tile([P, TILES, 2, HALF], FP32)
+        sin_q = const.tile([P, TILES, HALF, 2], FP32)
+        sin_k = const.tile([P, TILES, HALF, 2], FP32)
         sin_pairs = sin_bf[:].rearrange("p t (i m) -> p t i m", m=2)
         for table, factor in ((sin_q, Q_SCALE), (sin_k, 1.0)):
-            nc.gpsimd.tensor_scalar(
-                out=table[:, :, 0, :], in0=sin_pairs[:, :, :, 0], scalar1=-factor, scalar2=0.0, op0=ALU.mult, op1=ALU.add
-            )
-            nc.gpsimd.tensor_scalar(
-                out=table[:, :, 1, :], in0=sin_pairs[:, :, :, 1], scalar1=factor, scalar2=0.0, op0=ALU.mult, op1=ALU.add
-            )
+            for member, sign in ((0, -1.0), (1, 1.0)):
+                nc.gpsimd.tensor_scalar(
+                    out=table[:, :, :, member],
+                    in0=sin_pairs[:, :, :, member],
+                    scalar1=sign * factor,
+                    scalar2=0.0,
+                    op0=ALU.mult,
+                    op1=ALU.add,
+                )
 
         gamma_col = const.tile([P, K_BLOCKS], FP32)
         w_codes = const.tile([P, PASSES, W_COLS], U32, align_bytes=64)
@@ -155,23 +158,27 @@ def tile_attention_pa_t_kernel(tc, x, gamma, wq, wk, wv, sin, cos, out_0, out_1,
             std[b] = stat_pool.tile([P, TILES], FP32, name="std")
             nc.scalar.activation(out=std[b][:], in_=var_eps[:], func=ACT.Sqrt)
 
+        shift = {}
+
         def inverse_std(b):
             rstd[b] = stat_pool.tile([P, TILES], FP32, name="rstd")
             nc.vector.reciprocal(out=rstd[b][:], in_=std[b][:])
+            shift[b] = stat_pool.tile([P, TILES], FP32, name="shift")
+            nc.vector.tensor_tensor(out=shift[b][:], in0=neg_mean[b][:], in1=rstd[b][:], op=ALU.mult)
 
         y = {}
 
         def normalise(i):
             b, t = divmod(i, TILES)
             y[i] = y_pool.tile([P, D], FP32, name="y")
-            nc.gpsimd.tensor_scalar(
-                out=y[i][:],
-                in0=x_sb[b][:, t, :],
-                scalar1=neg_mean[b][:, t : t + 1],
-                scalar2=rstd[b][:, t : t + 1],
-                op0=ALU.add,
-                op1=ALU.mult,
-            )
+            row_rstd = rstd[b][:, t : t + 1]
+            row_shift = shift[b][:, t : t + 1]
+            if i % 2 == 0:
+                nc.gpsimd.tensor_scalar(
+                    out=y[i][:], in0=x_sb[b][:, t, :], scalar1=row_rstd, scalar2=row_shift, op0=ALU.mult, op1=ALU.add
+                )
+            else:
+                nc.scalar.activation(out=y[i][:], in_=x_sb[b][:, t, :], func=ACT.Identity, scale=row_rstd, bias=row_shift)
 
         xt = {}
         grouped = {}
@@ -232,34 +239,30 @@ def tile_attention_pa_t_kernel(tc, x, gamma, wq, wk, wv, sin, cos, out_0, out_1,
 
         def rotary_products(u, cos_table, sin_table, cos_out, sin_out):
             nc.vector.tensor_tensor(out=cos_out, in0=u, in1=cos_table, op=ALU.mult)
-            pairs = u.rearrange("p a (i m) -> p a i m", m=2)
-            for plane in range(2):
-                nc.vector.tensor_tensor(
-                    out=sin_out[:, :, plane, :], in0=pairs[:, :, :, 1 - plane], in1=sin_table[:, :, plane, :], op=ALU.mult
-                )
+            swapped = u.rearrange("p a (i m) -> p a i m", m=2)[:, :, :, ::-1]
+            nc.vector.tensor_tensor(
+                out=sin_out.rearrange("p a (i m) -> p a i m", m=2), in0=swapped, in1=sin_table, op=ALU.mult
+            )
 
         def rotary_sum(cos_out, sin_out):
-            interleaved = cos_out.rearrange("p a (i m) -> p a i m", m=2)
-            nc.gpsimd.tensor_tensor(
-                out=interleaved, in0=interleaved, in1=sin_out.rearrange("p a m i -> p a i m"), op=ALU.add
-            )
+            nc.gpsimd.tensor_tensor(out=cos_out, in0=cos_out, in1=sin_out, op=ALU.add)
 
         def rotate_q(i):
             b, t = divmod(i, TILES)
             if t == 0:
                 rotated[b] = out_pool.tile([P, HEADS, TILES, DH], FP32, name="rotated")
-                sin_part[b] = out_pool.tile([P, HEADS, TILES, 2, HALF], FP32, name="sin_part")
+                sin_part[b] = out_pool.tile([P, HEADS, TILES, DH], FP32, name="sin_part")
             rotary_products(
                 u=q_ps[i][:].rearrange("p (h d) -> p h d", h=H),
                 cos_table=cos_q[:, t, :].unsqueeze(1).to_broadcast([P, H, DH]),
-                sin_table=sin_q[:, t, :, :].unsqueeze(1).to_broadcast([P, H, 2, HALF]),
+                sin_table=sin_q[:, t, :, :].unsqueeze(1).to_broadcast([P, H, HALF, 2]),
                 cos_out=rotated[b][:, 0:H, t, :],
-                sin_out=sin_part[b][:, 0:H, t, :, :],
+                sin_out=sin_part[b][:, 0:H, t, :],
             )
 
         def sum_q(i):
             b, t = divmod(i, TILES)
-            rotary_sum(rotated[b][:, 0:H, t, :], sin_part[b][:, 0:H, t, :, :])
+            rotary_sum(rotated[b][:, 0:H, t, :], sin_part[b][:, 0:H, t, :])
 
         v_sb = {}
 
@@ -269,13 +272,13 @@ def tile_attention_pa_t_kernel(tc, x, gamma, wq, wk, wv, sin, cos, out_0, out_1,
                 cos_table=cos_bf[:],
                 sin_table=sin_k[:],
                 cos_out=rotated[b][:, H, :, :],
-                sin_out=sin_part[b][:, H, :, :, :],
+                sin_out=sin_part[b][:, H, :, :],
             )
             v_sb[b] = out_pool.tile([P, TILES, DH], FP32, name="v_sb")
             nc.scalar.copy(out=v_sb[b][:], in_=v_ps[b][:])
 
         def sum_k_and_store(b):
-            rotary_sum(rotated[b][:, H, :, :], sin_part[b][:, H, :, :, :])
+            rotary_sum(rotated[b][:, H, :, :], sin_part[b][:, H, :, :])
             nc.sync.dma_start(out=out_0[b].rearrange("h (p t) d -> p h t d", t=TILES), in_=rotated[b][:, 0:H, :, :])
             nc.sync.dma_start(out=out_1[b].rearrange("(p t) d -> p t d", t=TILES), in_=rotated[b][:, H, :, :])
             nc.sync.dma_start(out=out_2[b].rearrange("(p t) d -> p t d", t=TILES), in_=v_sb[b][:])

@@ -84,16 +84,18 @@ def tile_attention_pa_t_kernel(tc, x, gamma, wq, wk, wv, sin, cos, out_0, out_1,
         root_of_one = const.tile([P, 1], FP32)
         nc.scalar.activation(out=root_of_one[:], in_=one[:], func=ACT.Sqrt)
 
-        cos_q = const.tile([P, TILES, DH], FP32)
-        nc.gpsimd.tensor_scalar(out=cos_q[:], in0=cos_bf[:], scalar1=Q_SCALE, scalar2=0.0, op0=ALU.mult, op1=ALU.add)
-        sin_q = const.tile([P, TILES, HALF, 2], FP32)
-        sin_k = const.tile([P, TILES, HALF, 2], FP32)
+        table_q = const.tile([P, TILES, 2, DH], FP32)
+        table_k = const.tile([P, TILES, 2, DH], FP32)
         sin_pairs = sin_bf[:].rearrange("p t (i m) -> p t i m", m=2)
-        for table, factor in ((sin_q, Q_SCALE), (sin_k, 1.0)):
-            for member, sign in ((0, -1.0), (1, 1.0)):
+        for table, factor in ((table_q, Q_SCALE), (table_k, 1.0)):
+            nc.gpsimd.tensor_scalar(
+                out=table[:, :, 0, :], in0=cos_bf[:], scalar1=factor, scalar2=0.0, op0=ALU.mult, op1=ALU.add
+            )
+            partner_pairs = table[:, :, 1, :].rearrange("p t (i m) -> p t i m", m=2)
+            for member, sign in ((0, 1.0), (1, -1.0)):
                 nc.gpsimd.tensor_scalar(
-                    out=table[:, :, :, member],
-                    in0=sin_pairs[:, :, :, member],
+                    out=partner_pairs[:, :, :, member],
+                    in0=sin_pairs[:, :, :, 1 - member],
                     scalar1=sign * factor,
                     scalar2=0.0,
                     op0=ALU.mult,
@@ -234,53 +236,44 @@ def tile_attention_pa_t_kernel(tc, x, gamma, wq, wk, wv, sin, cos, out_0, out_1,
                         stop=(g == PASSES - 1),
                     )
 
-        rotated = {}
-        sin_part = {}
+        products = {}
 
-        def rotary_products(u, cos_table, sin_table, cos_out, sin_out):
-            nc.vector.tensor_tensor(out=cos_out, in0=u, in1=cos_table, op=ALU.mult)
-            swapped = u.rearrange("p a (i m) -> p a i m", m=2)[:, :, :, ::-1]
-            nc.vector.tensor_tensor(
-                out=sin_out.rearrange("p a (i m) -> p a i m", m=2), in0=swapped, in1=sin_table, op=ALU.mult
-            )
+        def rotary_products(u, table, out):
+            nc.vector.tensor_tensor(out=out, in0=u.unsqueeze(1).to_broadcast(out.shape), in1=table, op=ALU.mult)
 
-        def rotary_sum(cos_out, sin_out):
-            nc.gpsimd.tensor_tensor(out=cos_out, in0=cos_out, in1=sin_out, op=ALU.add)
+        def rotary_sum(both):
+            result = both[:, 0, :, :].rearrange("p a (i m) -> p a i m", m=2)
+            partner = both[:, 1, :, :].rearrange("p a (i m) -> p a i m", m=2)[:, :, :, ::-1]
+            nc.gpsimd.tensor_tensor(out=result, in0=result, in1=partner, op=ALU.add)
 
         def rotate_q(i):
             b, t = divmod(i, TILES)
             if t == 0:
-                rotated[b] = out_pool.tile([P, HEADS, TILES, DH], FP32, name="rotated")
-                sin_part[b] = out_pool.tile([P, HEADS, TILES, DH], FP32, name="sin_part")
+                products[b] = out_pool.tile([P, 2, HEADS, TILES, DH], FP32, name="products")
             rotary_products(
                 u=q_ps[i][:].rearrange("p (h d) -> p h d", h=H),
-                cos_table=cos_q[:, t, :].unsqueeze(1).to_broadcast([P, H, DH]),
-                sin_table=sin_q[:, t, :, :].unsqueeze(1).to_broadcast([P, H, HALF, 2]),
-                cos_out=rotated[b][:, 0:H, t, :],
-                sin_out=sin_part[b][:, 0:H, t, :],
+                table=table_q[:, t, :, :].unsqueeze(2).to_broadcast([P, 2, H, DH]),
+                out=products[b][:, :, 0:H, t, :],
             )
 
         def sum_q(i):
             b, t = divmod(i, TILES)
-            rotary_sum(rotated[b][:, 0:H, t, :], sin_part[b][:, 0:H, t, :])
+            rotary_sum(products[b][:, :, 0:H, t, :])
 
         v_sb = {}
 
         def rotate_k_copy_v(b):
             rotary_products(
-                u=k_ps[b][:],
-                cos_table=cos_bf[:],
-                sin_table=sin_k[:],
-                cos_out=rotated[b][:, H, :, :],
-                sin_out=sin_part[b][:, H, :, :],
+                u=k_ps[b][:], table=table_k[:].rearrange("p t c d -> p c t d"), out=products[b][:, :, H, :, :]
             )
             v_sb[b] = out_pool.tile([P, TILES, DH], FP32, name="v_sb")
             nc.scalar.copy(out=v_sb[b][:], in_=v_ps[b][:])
 
         def sum_k_and_store(b):
-            rotary_sum(rotated[b][:, H, :, :], sin_part[b][:, H, :, :])
-            nc.sync.dma_start(out=out_0[b].rearrange("h (p t) d -> p h t d", t=TILES), in_=rotated[b][:, 0:H, :, :])
-            nc.sync.dma_start(out=out_1[b].rearrange("(p t) d -> p t d", t=TILES), in_=rotated[b][:, H, :, :])
+            rotary_sum(products[b][:, :, H, :, :])
+            result = products[b][:, 0, :, :, :]
+            nc.sync.dma_start(out=out_0[b].rearrange("h (p t) d -> p h t d", t=TILES), in_=result[:, 0:H, :, :])
+            nc.sync.dma_start(out=out_1[b].rearrange("(p t) d -> p t d", t=TILES), in_=result[:, H, :, :])
             nc.sync.dma_start(out=out_2[b].rearrange("(p t) d -> p t d", t=TILES), in_=v_sb[b][:])
 
         def is_tile(i):

@@ -84,18 +84,16 @@ def tile_attention_pa_t_kernel(tc, x, gamma, wq, wk, wv, sin, cos, out_0, out_1,
         root_of_one = const.tile([P, 1], FP32)
         nc.scalar.activation(out=root_of_one[:], in_=one[:], func=ACT.Sqrt)
 
-        table_q = const.tile([P, TILES, 2, DH], FP32)
-        table_k = const.tile([P, TILES, 2, DH], FP32)
+        cos_q = const.tile([P, TILES, DH], FP32)
+        nc.gpsimd.tensor_scalar(out=cos_q[:], in0=cos_bf[:], scalar1=Q_SCALE, scalar2=0.0, op0=ALU.mult, op1=ALU.add)
+        sin_q = const.tile([P, TILES, HALF, 2], FP32)
+        sin_k = const.tile([P, TILES, HALF, 2], FP32)
         sin_pairs = sin_bf[:].rearrange("p t (i m) -> p t i m", m=2)
-        for table, factor in ((table_q, Q_SCALE), (table_k, 1.0)):
-            nc.gpsimd.tensor_scalar(
-                out=table[:, :, 0, :], in0=cos_bf[:], scalar1=factor, scalar2=0.0, op0=ALU.mult, op1=ALU.add
-            )
-            partner_pairs = table[:, :, 1, :].rearrange("p t (i m) -> p t i m", m=2)
-            for member, sign in ((0, 1.0), (1, -1.0)):
+        for table, factor in ((sin_q, Q_SCALE), (sin_k, 1.0)):
+            for member, sign in ((0, -1.0), (1, 1.0)):
                 nc.gpsimd.tensor_scalar(
-                    out=partner_pairs[:, :, :, member],
-                    in0=sin_pairs[:, :, :, 1 - member],
+                    out=table[:, :, :, member],
+                    in0=sin_pairs[:, :, :, member],
                     scalar1=sign * factor,
                     scalar2=0.0,
                     op0=ALU.mult,
@@ -175,7 +173,7 @@ def tile_attention_pa_t_kernel(tc, x, gamma, wq, wk, wv, sin, cos, out_0, out_1,
             y[i] = y_pool.tile([P, D], FP32, name="y")
             row_rstd = rstd[b][:, t : t + 1]
             row_shift = shift[b][:, t : t + 1]
-            if i % 2 == 0:
+            if t != TILES - 1:
                 nc.gpsimd.tensor_scalar(
                     out=y[i][:], in0=x_sb[b][:, t, :], scalar1=row_rstd, scalar2=row_shift, op0=ALU.mult, op1=ALU.add
                 )
@@ -236,44 +234,53 @@ def tile_attention_pa_t_kernel(tc, x, gamma, wq, wk, wv, sin, cos, out_0, out_1,
                         stop=(g == PASSES - 1),
                     )
 
-        products = {}
+        rotated = {}
+        sin_part = {}
 
-        def rotary_products(u, table, out):
-            nc.vector.tensor_tensor(out=out, in0=u.unsqueeze(1).to_broadcast(out.shape), in1=table, op=ALU.mult)
+        def rotary_products(u, cos_table, sin_table, cos_out, sin_out):
+            nc.vector.tensor_tensor(out=cos_out, in0=u, in1=cos_table, op=ALU.mult)
+            swapped = u.rearrange("p a (i m) -> p a i m", m=2)[:, :, :, ::-1]
+            nc.vector.tensor_tensor(
+                out=sin_out.rearrange("p a (i m) -> p a i m", m=2), in0=swapped, in1=sin_table, op=ALU.mult
+            )
 
-        def rotary_sum(both):
-            result = both[:, 0, :, :].rearrange("p a (i m) -> p a i m", m=2)
-            partner = both[:, 1, :, :].rearrange("p a (i m) -> p a i m", m=2)[:, :, :, ::-1]
-            nc.gpsimd.tensor_tensor(out=result, in0=result, in1=partner, op=ALU.add)
+        def rotary_sum(cos_out, sin_out):
+            nc.gpsimd.tensor_tensor(out=cos_out, in0=cos_out, in1=sin_out, op=ALU.add)
 
         def rotate_q(i):
             b, t = divmod(i, TILES)
             if t == 0:
-                products[b] = out_pool.tile([P, 2, HEADS, TILES, DH], FP32, name="products")
+                rotated[b] = out_pool.tile([P, HEADS, TILES, DH], FP32, name="rotated")
+                sin_part[b] = out_pool.tile([P, HEADS, TILES, DH], FP32, name="sin_part")
             rotary_products(
                 u=q_ps[i][:].rearrange("p (h d) -> p h d", h=H),
-                table=table_q[:, t, :, :].unsqueeze(2).to_broadcast([P, 2, H, DH]),
-                out=products[b][:, :, 0:H, t, :],
+                cos_table=cos_q[:, t, :].unsqueeze(1).to_broadcast([P, H, DH]),
+                sin_table=sin_q[:, t, :, :].unsqueeze(1).to_broadcast([P, H, HALF, 2]),
+                cos_out=rotated[b][:, 0:H, t, :],
+                sin_out=sin_part[b][:, 0:H, t, :],
             )
 
         def sum_q(i):
             b, t = divmod(i, TILES)
-            rotary_sum(products[b][:, :, 0:H, t, :])
+            rotary_sum(rotated[b][:, 0:H, t, :], sin_part[b][:, 0:H, t, :])
 
         v_sb = {}
 
         def rotate_k_copy_v(b):
             rotary_products(
-                u=k_ps[b][:], table=table_k[:].rearrange("p t c d -> p c t d"), out=products[b][:, :, H, :, :]
+                u=k_ps[b][:],
+                cos_table=cos_bf[:],
+                sin_table=sin_k[:],
+                cos_out=rotated[b][:, H, :, :],
+                sin_out=sin_part[b][:, H, :, :],
             )
             v_sb[b] = out_pool.tile([P, TILES, DH], FP32, name="v_sb")
             nc.scalar.copy(out=v_sb[b][:], in_=v_ps[b][:])
 
         def sum_k_and_store(b):
-            rotary_sum(products[b][:, :, H, :, :])
-            result = products[b][:, 0, :, :, :]
-            nc.sync.dma_start(out=out_0[b].rearrange("h (p t) d -> p h t d", t=TILES), in_=result[:, 0:H, :, :])
-            nc.sync.dma_start(out=out_1[b].rearrange("(p t) d -> p t d", t=TILES), in_=result[:, H, :, :])
+            rotary_sum(rotated[b][:, H, :, :], sin_part[b][:, H, :, :])
+            nc.sync.dma_start(out=out_0[b].rearrange("h (p t) d -> p h t d", t=TILES), in_=rotated[b][:, 0:H, :, :])
+            nc.sync.dma_start(out=out_1[b].rearrange("(p t) d -> p t d", t=TILES), in_=rotated[b][:, H, :, :])
             nc.sync.dma_start(out=out_2[b].rearrange("(p t) d -> p t d", t=TILES), in_=v_sb[b][:])
 
         def is_tile(i):

from contextlib import ExitStack

import concourse.mybir as mybir
from concourse.masks import make_identity

FP32 = mybir.dt.float32
BF16 = mybir.dt.bfloat16
U32 = mybir.dt.uint32
U8 = mybir.dt.uint8
FP8X4 = mybir.dt.float8_e4m3fn_x4
ALU = mybir.AluOpType
ACT = mybir.ActivationFunctionType

B, N, D, H, DH = 8, 512, 1024, 4, 128
EPS = 1e-5
Q_SCALE = DH**-0.5

P = 128
PACK = 4
PASSES = D // (P * PACK)
K_BLOCKS = D // P
TILES = N // P
ROW_TILES = B * TILES
HEADS = H + 1
HALF = DH // 2
Q_COLS = slice(0, H * DH)
K_COLS = slice(H * DH, H * DH + DH)
V_COLS = slice(H * DH + DH, H * DH + 2 * DH)
KV_COLS = slice(H * DH, H * DH + 2 * DH)
W_COLS = H * DH + 2 * DH

SUM_LEAD = 8
STAT_LEAD = 5
Y_LEAD = 4
T_LEAD = 3
G_LEAD = 2
MX_LEAD = 1
VECTOR_SUM_ENTRIES = 1

FLOPS = 2 * B * N * D * W_COLS


def tile_attention_pa_t_kernel(tc, x, gamma, wq, wk, wv, sin, cos, out_0, out_1, out_2):
    nc = tc.nc
    with ExitStack() as ctx:
        const = ctx.enter_context(tc.tile_pool(name="const", bufs=1))
        x_pool = ctx.enter_context(tc.tile_pool(name="x_pool", bufs=B))
        stat_pool = ctx.enter_context(tc.tile_pool(name="stat_pool", bufs=3))
        unread_pool = ctx.enter_context(tc.tile_pool(name="unread_pool", bufs=4))
        y_pool = ctx.enter_context(tc.tile_pool(name="y_pool", bufs=4))
        mx_pool = ctx.enter_context(tc.tile_pool(name="mx_pool", bufs=3))
        out_pool = ctx.enter_context(tc.tile_pool(name="out_pool", bufs=2))
        xt_psum = ctx.enter_context(tc.psum_pool(name="xt_psum", bufs=2))
        qkv_psum = ctx.enter_context(tc.psum_pool(name="qkv_psum", bufs=2))

        ident = const.tile([P, P], FP32)
        make_identity(nc, ident[:])

        ctx.enter_context(tc.manual_schedule())

        x_sb = [x_pool.tile([P, TILES, D], BF16, name="x_sb") for b in range(B)]

        def load_x(b):
            nc.sync.dma_start(out=x_sb[b][:], in_=x[b].rearrange("(p t) k -> p t k", t=TILES))

        load_x(0)
        load_x(1)
        w_raw = const.tile([P, K_BLOCKS, W_COLS], BF16)
        nc.sync.dma_start(out=w_raw[:, :, Q_COLS], in_=wq.rearrange("(j p) n -> p j n", p=P))
        nc.sync.dma_start(out=w_raw[:, :, K_COLS], in_=wk.rearrange("(j p) n -> p j n", p=P))
        nc.sync.dma_start(out=w_raw[:, :, V_COLS], in_=wv.rearrange("(j p) n -> p j n", p=P))
        gamma_rows = const.tile([P, P], BF16)
        nc.vector.memset(gamma_rows[:], 0.0)
        nc.sync.dma_start(out=gamma_rows[0:K_BLOCKS, :], in_=gamma.rearrange("(j p) -> j p", p=P))
        cos_bf = const.tile([P, TILES, DH], BF16)
        sin_bf = const.tile([P, TILES, DH], BF16)
        nc.sync.dma_start(out=cos_bf[:], in_=cos.rearrange("(p t) d -> p t d", t=TILES))
        nc.sync.dma_start(out=sin_bf[:], in_=sin.rearrange("(p t) d -> p t d", t=TILES))
        for b in range(2, B):
            load_x(b)

        one = const.tile([P, 1], FP32)
        nc.vector.memset(one[:], 1.0)
        root_of_one = const.tile([P, 1], FP32)
        nc.scalar.activation(out=root_of_one[:], in_=one[:], func=ACT.Sqrt)

        cos_q = const.tile([P, TILES, DH], FP32)
        nc.gpsimd.tensor_scalar(out=cos_q[:], in0=cos_bf[:], scalar1=Q_SCALE, scalar2=0.0, op0=ALU.mult, op1=ALU.add)
        sin_q = const.tile([P, TILES, HALF, 2], FP32)
        sin_k = const.tile([P, TILES, HALF, 2], FP32)
        sin_pairs = sin_bf[:].rearrange("p t (i m) -> p t i m", m=2)
        for table, factor in ((sin_q, Q_SCALE), (sin_k, 1.0)):
            for member, sign in ((0, -1.0), (1, 1.0)):
                nc.gpsimd.tensor_scalar(
                    out=table[:, :, :, member],
                    in0=sin_pairs[:, :, :, member],
                    scalar1=sign * factor,
                    scalar2=0.0,
                    op0=ALU.mult,
                    op1=ALU.add,
                )

        gamma_col = const.tile([P, K_BLOCKS], FP32)
        w_codes = const.tile([P, PASSES, W_COLS], U32, align_bytes=64)
        w_scales = const.tile([P, PASSES, W_COLS], U8, align_bytes=64)

        def prepare_gamma_and_weights():
            gamma_rows_f = const.tile([P, P], FP32)
            nc.vector.tensor_copy(out=gamma_rows_f[:], in_=gamma_rows[:])
            gamma_ps = xt_psum.tile([P, PACK, P], FP32, name="xt")
            nc.tensor.transpose(gamma_ps[:, 0, :], gamma_rows_f[:], ident[:])
            nc.vector.tensor_copy(out=gamma_col[:], in_=gamma_ps[:, 0, 0:K_BLOCKS])
            w_grouped = [
                const.tile([P, W_COLS, PACK], BF16, name="w_grouped%d" % g, align_bytes=64) for g in range(PASSES)
            ]
            for g in range(PASSES):
                nc.vector.tensor_copy(
                    out=w_grouped[g][:], in_=w_raw[:, g * PACK : (g + 1) * PACK, :].rearrange("p j n -> p n j")
                )
            for g in range(PASSES):
                for cols in (Q_COLS, KV_COLS):
                    nc.vector.quantize_mx(
                        out=w_codes[:, g, cols].bitcast(FP8X4),
                        scales=w_scales[:, g, cols],
                        in_=w_grouped[g][:, cols, :].rearrange("p n j -> p (n j)"),
                    )

        sums = {}
        squares = {}

        def row_sums(i):
            b, t = divmod(i, TILES)
            if t == 0:
                sums[b] = stat_pool.tile([P, TILES], FP32, name="sums")
                squares[b] = stat_pool.tile([P, TILES], FP32, name="squares")
                if b < VECTOR_SUM_ENTRIES:
                    nc.vector.tensor_reduce(out=sums[b][:], in_=x_sb[b][:], axis=mybir.AxisListType.X, op=ALU.add)
            scalar_work = [(ACT.Square, squares[b])] + ([(ACT.Identity, sums[b])] if b >= VECTOR_SUM_ENTRIES else [])
            for func, total in scalar_work:
                unread = unread_pool.tile([P, D], BF16, name="unread")
                nc.scalar.activation(out=unread[:], in_=x_sb[b][:, t, :], func=func, accum_out=total[:, t : t + 1])

        neg_mean = {}
        std = {}
        rstd = {}

        def variance(b):
            neg_mean[b] = stat_pool.tile([P, TILES], FP32, name="neg_mean")
            nc.vector.tensor_scalar_mul(out=neg_mean[b][:], in0=sums[b][:], scalar1=-1.0 / D)
            mean_sq = stat_pool.tile([P, TILES], FP32, name="mean_sq")
            nc.vector.tensor_tensor(out=mean_sq[:], in0=neg_mean[b][:], in1=neg_mean[b][:], op=ALU.mult)
            second = stat_pool.tile([P, TILES], FP32, name="second")
            nc.vector.tensor_scalar(
                out=second[:], in0=squares[b][:], scalar1=1.0 / D, scalar2=EPS, op0=ALU.mult, op1=ALU.add
            )
            var_eps = stat_pool.tile([P, TILES], FP32, name="var_eps")
            nc.vector.tensor_tensor(out=var_eps[:], in0=second[:], in1=mean_sq[:], op=ALU.subtract)
            std[b] = stat_pool.tile([P, TILES], FP32, name="std")
            nc.scalar.activation(out=std[b][:], in_=var_eps[:], func=ACT.Sqrt)

        shift = {}

        def inverse_std(b):
            rstd[b] = stat_pool.tile([P, TILES], FP32, name="rstd")
            nc.vector.reciprocal(out=rstd[b][:], in_=std[b][:])
            shift[b] = stat_pool.tile([P, TILES], FP32, name="shift")
            nc.vector.tensor_tensor(out=shift[b][:], in0=neg_mean[b][:], in1=rstd[b][:], op=ALU.mult)

        y = {}

        def normalise(i):
            b, t = divmod(i, TILES)
            y[i] = y_pool.tile([P, D], FP32, name="y")
            row_rstd = rstd[b][:, t : t + 1]
            row_shift = shift[b][:, t : t + 1]
            if t != TILES - 1:
                nc.gpsimd.tensor_scalar(
                    out=y[i][:], in0=x_sb[b][:, t, :], scalar1=row_rstd, scalar2=row_shift, op0=ALU.mult, op1=ALU.add
                )
            else:
                nc.scalar.activation(out=y[i][:], in_=x_sb[b][:, t, :], func=ACT.Identity, scale=row_rstd, bias=row_shift)

        xt = {}
        grouped = {}

        def transpose(i):
            xt[i] = [xt_psum.tile([P, PACK, P], FP32, name="xt") for g in range(PASSES)]
            for g in range(PASSES):
                for j in range(PACK):
                    block = g * PACK + j
                    nc.tensor.transpose(xt[i][g][:, j, :], y[i][:, block * P : (block + 1) * P], ident[:])

        def scale_by_gamma(i):
            grouped[i] = mx_pool.tile([P, PASSES, P, PACK], BF16, name="grouped", align_bytes=64)
            for g in range(PASSES):
                nc.vector.tensor_tensor(
                    out=grouped[i][:, g, :, :],
                    in0=xt[i][g][:].rearrange("p j r -> p r j"),
                    in1=gamma_col[:, g * PACK : (g + 1) * PACK].unsqueeze(1).to_broadcast([P, P, PACK]),
                    op=ALU.mult,
                )

        codes = {}
        scales = {}

        def quantise(i):
            codes[i] = mx_pool.tile([P, PASSES, P], U32, name="codes", align_bytes=64)
            scales[i] = mx_pool.tile([P, PASSES, P], U8, name="scales", align_bytes=64)
            nc.vector.quantize_mx(
                out=codes[i][:].rearrange("p g r -> p (g r)").bitcast(FP8X4),
                scales=scales[i][:].rearrange("p g r -> p (g r)"),
                in_=grouped[i][:].rearrange("p g r j -> p (g r j)"),
            )

        q_ps = {}
        k_ps = {}
        v_ps = {}

        def project(i):
            b, t = divmod(i, TILES)
            q_ps[i] = qkv_psum.tile([P, H * DH], FP32, name="q_ps")
            if t == 0:
                k_ps[b] = qkv_psum.tile([P, TILES, DH], FP32, name="k_ps")
                v_ps[b] = qkv_psum.tile([P, TILES, DH], FP32, name="v_ps")
            for acc, cols in ((q_ps[i][:], Q_COLS), (k_ps[b][:, t, :], K_COLS), (v_ps[b][:, t, :], V_COLS)):
                for g in range(PASSES):
                    nc.tensor.matmul_mx(
                        out=acc,
                        lhsT=codes[i][:, g, :].bitcast(FP8X4),
                        lhsT_scale=scales[i][:, g, :],
                        rhs=w_codes[:, g, cols].bitcast(FP8X4),
                        rhs_scale=w_scales[:, g, cols],
                        start=(g == 0),
                        stop=(g == PASSES - 1),
                    )

        rotated = {}
        sin_part = {}

        def rotary_products(u, cos_table, sin_table, cos_out, sin_out):
            nc.vector.tensor_tensor(out=cos_out, in0=u, in1=cos_table, op=ALU.mult)
            swapped = u.rearrange("p a (i m) -> p a i m", m=2)[:, :, :, ::-1]
            nc.vector.tensor_tensor(
                out=sin_out.rearrange("p a (i m) -> p a i m", m=2), in0=swapped, in1=sin_table, op=ALU.mult
            )

        def rotary_sum(cos_out, sin_out):
            nc.gpsimd.tensor_tensor(out=cos_out, in0=cos_out, in1=sin_out, op=ALU.add)

        def rotate_q(i):
            b, t = divmod(i, TILES)
            if t == 0:
                rotated[b] = out_pool.tile([P, HEADS, TILES, DH], FP32, name="rotated")
                sin_part[b] = out_pool.tile([P, HEADS, TILES, DH], FP32, name="sin_part")
            rotary_products(
                u=q_ps[i][:].rearrange("p (h d) -> p h d", h=H),
                cos_table=cos_q[:, t, :].unsqueeze(1).to_broadcast([P, H, DH]),
                sin_table=sin_q[:, t, :, :].unsqueeze(1).to_broadcast([P, H, HALF, 2]),
                cos_out=rotated[b][:, 0:H, t, :],
                sin_out=sin_part[b][:, 0:H, t, :],
            )

        def sum_q(i):
            b, t = divmod(i, TILES)
            rotary_sum(rotated[b][:, 0:H, t, :], sin_part[b][:, 0:H, t, :])

        v_sb = {}

        def rotate_k_copy_v(b):
            rotary_products(
                u=k_ps[b][:],
                cos_table=cos_bf[:],
                sin_table=sin_k[:],
                cos_out=rotated[b][:, H, :, :],
                sin_out=sin_part[b][:, H, :, :],
            )
            v_sb[b] = out_pool.tile([P, TILES, DH], FP32, name="v_sb")
            nc.scalar.copy(out=v_sb[b][:], in_=v_ps[b][:])

        def sum_k_and_store(b):
            rotary_sum(rotated[b][:, H, :, :], sin_part[b][:, H, :, :])
            nc.sync.dma_start(out=out_0[b].rearrange("h (p t) d -> p h t d", t=TILES), in_=rotated[b][:, 0:H, :, :])
            nc.sync.dma_start(out=out_1[b].rearrange("(p t) d -> p t d", t=TILES), in_=rotated[b][:, H, :, :])
            nc.sync.dma_start(out=out_2[b].rearrange("(p t) d -> p t d", t=TILES), in_=v_sb[b][:])

        def is_tile(i):
            return 0 <= i < ROW_TILES

        def starts_entry(i):
            return is_tile(i) and i % TILES == 0

        def ends_entry(i):
            return is_tile(i) and i % TILES == TILES - 1

        for s in range(-SUM_LEAD, ROW_TILES + 1):
            if is_tile(s - 1):
                sum_q(s - 1)
            if ends_entry(s - 1):
                sum_k_and_store((s - 1) // TILES)
            if is_tile(s + SUM_LEAD):
                row_sums(s + SUM_LEAD)
            if is_tile(s + MX_LEAD):
                project(s + MX_LEAD)
            if is_tile(s + G_LEAD):
                scale_by_gamma(s + G_LEAD)
            if is_tile(s + T_LEAD):
                transpose(s + T_LEAD)
            if starts_entry(s + STAT_LEAD - 1):
                inverse_std((s + STAT_LEAD - 1) // TILES)
            if is_tile(s + Y_LEAD):
                normalise(s + Y_LEAD)
            if s + Y_LEAD == 0:
                prepare_gamma_and_weights()
            if is_tile(s):
                rotate_q(s)
            if ends_entry(s):
                rotate_k_copy_v(s // TILES)
            if is_tile(s + G_LEAD):
                quantise(s + G_LEAD)
            if starts_entry(s + STAT_LEAD):
                variance((s + STAT_LEAD) // TILES)
